import numpy as np
import ml_dtypes


def mxq(x, axis, fmt="e4m3"):
    dtype, down = {"e4m3": (ml_dtypes.float8_e4m3fn, 7), "e5m2": (ml_dtypes.float8_e5m2, 14)}[fmt]
    v = np.moveaxis(np.asarray(x, np.float32).astype(ml_dtypes.bfloat16).astype(np.float64), axis, -1)
    blocks = v.reshape(v.shape[:-1] + (-1, 32))
    amax = np.abs(blocks).max(-1, keepdims=True)
    byte = np.maximum(np.where(amax > 0, np.frexp(amax)[1] - 1 + 127, 0) - down, 1)
    scale = np.exp2(byte - 127.0)
    codes = (blocks / scale).astype(np.float32).astype(dtype).astype(np.float64)
    return np.moveaxis((codes * scale).reshape(v.shape), -1, axis)


WIDE = False


def mx_kscale(k):
    if not WIDE:
        return np.ones(k)
    levels = np.array([10, -10, 5, -5, 0])
    a = np.random.permutation(np.resize(levels, k // 512 * 4)).reshape(k // 512, 4)
    idx = np.arange(k)
    return np.exp2(a[idx // 512, idx % 128 // 32])


BF16 = ml_dtypes.bfloat16


def bf(x):
    return np.asarray(x, np.float32).astype(BF16)


def f64(x):
    return np.asarray(x).astype(np.float64)


B, T, C, KW = 4, 1024, 1024, 3
PAD = KW // 2


def setup_inputs():
    s = mx_kscale(C)
    return {"x": bf(np.random.standard_normal((B, T, C)) * s),
            "w1": bf(np.random.standard_normal((C, C)) / np.sqrt(C) / s[None, :]),
            "b1": bf(np.random.standard_normal(C) * 0.2),
            "w2": bf(np.random.standard_normal((C, KW)) * 0.8),
            "b2": bf(np.random.standard_normal(C) * 0.2)}


def reference(x, w1, b1, w2, b2):
    h = (mxq(f64(x), 2, "e4m3") @ mxq(f64(w1), 1, "e4m3").T) + f64(b1)
    hp = np.pad(h, ((0, 0), (PAD, PAD), (0, 0)))
    taps = f64(w2)
    y = hp[:, 0:T, :] * taps[:, 0]
    for j in range(1, KW):
        y = y + hp[:, j:j + T, :] * taps[:, j]
    return y + f64(b2)

@@ -1,0 +1,244 @@
+from contextlib import ExitStack
+
+import concourse.mybir as mybir
+from concourse.masks import make_identity
+
+F32 = mybir.dt.float32
+BF16 = mybir.dt.bfloat16
+U32 = mybir.dt.uint32
+U8 = mybir.dt.uint8
+FP8X4 = mybir.dt.float8_e4m3fn_x4
+ALU = mybir.AluOpType
+ACT = mybir.ActivationFunctionType
+
+B, T, C, D, KW = 4, 1024, 1024, 1024, 3
+P = 128
+PACK = 4
+K_PASS = P * PACK
+PASSES = C // K_PASS
+PAIRS = PACK // 2
+N_MOVE = 512
+T_HALVES = T // N_MOVE
+T_BLOCKS = T // P
+HALF_BLOCKS = N_MOVE // P
+D_TILES = D // P
+BANK_TILES = N_MOVE // P
+LOAD_BLOCKS = 2
+
+X_AHEAD = T_BLOCKS + 2
+W_AHEAD = 2
+Y_LAG = T_BLOCKS + 1
+CONV_STEPS = B * D_TILES
+
+FLOPS = 2 * B * T * C * D + 2 * KW * B * T * D
+
+
+def flip_block(nc, flips, ident, words, grouped_words, copy):
+    flipped = flips.tile([P, PASSES, PAIRS, P], F32, tag="flip")
+    for g in range(PASSES):
+        for u in range(PAIRS):
+            first = (g * PAIRS + u) * P
+            nc.tensor.transpose(flipped[:, g, u, :], words[:, first : first + P], ident[:])
+    copy(out=grouped_words, in_=flipped[:].rearrange("p g u r -> p g r u"))
+
+
+def tile_cvim_pa_t_kernel(tc, x, w1, b1, w2, b2, out):
+    nc = tc.nc
+    with ExitStack() as pools:
+        consts = pools.enter_context(tc.tile_pool(name="consts", bufs=1))
+        raws = pools.enter_context(tc.tile_pool(name="raws", bufs=1))
+        groups = pools.enter_context(tc.tile_pool(name="groups", bufs=2))
+        codes = pools.enter_context(tc.tile_pool(name="codes", bufs=2 * T_HALVES))
+        ys = pools.enter_context(tc.tile_pool(name="ys", bufs=D_TILES + Y_LAG))
+        outs = pools.enter_context(tc.tile_pool(name="outs", bufs=4))
+        accs = pools.enter_context(tc.psum_pool(name="accs", bufs=4))
+        flips = pools.enter_context(tc.psum_pool(name="flips", bufs=2))
+        backs = pools.enter_context(tc.psum_pool(name="backs", bufs=2))
+
+        ident = consts.tile([P, P], F32)
+        make_identity(nc, ident[:])
+
+        x_raw = [raws.tile([P, T_BLOCKS * C], BF16, name="x_raw%d" % b) for b in range(B)]
+        w_raw = raws.tile([P, D_TILES * C], BF16)
+
+        def load_rows(raw, rows, first):
+            nc.sync.dma_start(
+                out=raw[:].rearrange("p (k c) -> p k c", c=C)[:, first : first + LOAD_BLOCKS, :],
+                in_=rows[first * P : (first + LOAD_BLOCKS) * P, :].rearrange("(k p) c -> p k c", p=P),
+            )
+
+        rows_bf16 = consts.tile([P, (2 + KW) * P], BF16)
+        nc.vector.memset(rows_bf16[:], 0.0)
+        nc.scalar.dma_start(out=rows_bf16[0:D_TILES, 0:P], in_=b1.rearrange("(e p) -> e p", p=P))
+        nc.scalar.dma_start(out=rows_bf16[0:D_TILES, P : 2 * P], in_=b2.rearrange("(e p) -> e p", p=P))
+        nc.scalar.dma_start(
+            out=rows_bf16[0:D_TILES, 2 * P : (2 + KW) * P], in_=w2.rearrange("(e p) j -> e (p j)", p=P)
+        )
+
+        load_rows(x_raw[0], x[0], 0)
+        load_rows(x_raw[0], x[0], 2)
+        load_rows(w_raw, w1, 0)
+        load_rows(x_raw[0], x[0], 4)
+        load_rows(x_raw[0], x[0], 6)
+        load_rows(x_raw[1], x[1], 0)
+        for first in range(LOAD_BLOCKS, D_TILES, LOAD_BLOCKS):
+            load_rows(w_raw, w1, first)
+        for first in range(LOAD_BLOCKS, T_BLOCKS, LOAD_BLOCKS):
+            load_rows(x_raw[1], x[1], first)
+        for b in range(2, B):
+            for first in range(0, T_BLOCKS, LOAD_BLOCKS):
+                load_rows(x_raw[b], x[b], first)
+
+        rows_f32 = consts.tile([P, 2 + KW, P], F32)
+        nc.vector.tensor_copy(
+            out=rows_f32[:, 0:2, :], in_=rows_bf16[:, 0 : 2 * P].rearrange("e (v p) -> e v p", v=2)
+        )
+        nc.vector.tensor_copy(
+            out=rows_f32[:, 2 : 2 + KW, :],
+            in_=rows_bf16[:, 2 * P : (2 + KW) * P].rearrange("e (p j) -> e j p", j=KW),
+        )
+        chan = consts.tile([P, 2 + KW, D_TILES], F32)
+        for v in range(2 + KW):
+            column = flips.tile([P, P], F32, tag="flip")
+            nc.tensor.transpose(column[:], rows_f32[:, v, :], ident[:])
+            nc.vector.tensor_copy(out=chan[:, v, :], in_=column[:, 0:D_TILES])
+        bias1 = chan[:, 0, :]
+        bias2 = chan[:, 1, :]
+        tap_sum = consts.tile([P, D_TILES], F32)
+        nc.vector.tensor_tensor(out=tap_sum[:], in0=chan[:, 2, :], in1=chan[:, 3, :], op=ALU.add)
+        nc.vector.tensor_tensor(out=tap_sum[:], in0=tap_sum[:], in1=chan[:, 4, :], op=ALU.add)
+        bias_all = consts.tile([P, D_TILES], F32)
+        nc.vector.tensor_tensor(out=bias_all[:], in0=tap_sum[:], in1=bias1, op=ALU.mult)
+        nc.vector.tensor_tensor(out=bias_all[:], in0=bias_all[:], in1=bias2, op=ALU.add)
+        edge_fix = consts.tile([P, D_TILES, 2], F32)
+        for side in range(2):
+            nc.vector.scalar_tensor_tensor(
+                out=edge_fix[:, :, side],
+                in0=bias1,
+                scalar=-1.0,
+                in1=chan[:, 2 + side * (KW - 1), :],
+                op0=ALU.mult,
+                op1=ALU.mult,
+            )
+
+        w_codes = consts.tile([P, D_TILES * PASSES * P], U32, align_bytes=64)
+        w_scales = consts.tile([P, D_TILES * PASSES * P], U8, align_bytes=64)
+
+        def prepare_w(e):
+            w_grouped = groups.tile([P, PASSES * P * PACK], BF16, align_bytes=64)
+            flip_block(
+                nc,
+                flips,
+                ident,
+                w_raw[:].bitcast(F32)[:, e * (C // 2) : (e + 1) * (C // 2)],
+                w_grouped[:].bitcast(F32).rearrange("p (g r u) -> p g r u", g=PASSES, u=PAIRS),
+                nc.scalar.copy,
+            )
+            cols = slice(e * PASSES * P, (e + 1) * PASSES * P)
+            nc.vector.quantize_mx(
+                out=w_codes[:, cols].bitcast(FP8X4), scales=w_scales[:, cols], in_=w_grouped[:]
+            )
+
+        x_grouped = {}
+        x_codes = {}
+        x_scales = {}
+
+        def prepare_x(n):
+            half, q = divmod(n, HALF_BLOCKS)
+            b, k = divmod(n, T_BLOCKS)
+            if q == 0:
+                x_grouped[half] = groups.tile(
+                    [P, PASSES * N_MOVE * PACK], BF16, align_bytes=64, name="x_grouped"
+                )
+            flip_block(
+                nc,
+                flips,
+                ident,
+                x_raw[b][:].bitcast(F32)[:, k * (C // 2) : (k + 1) * (C // 2)],
+                x_grouped[half][:]
+                .bitcast(F32)
+                .rearrange("p (g t u) -> p g t u", g=PASSES, u=PAIRS)[:, :, q * P : (q + 1) * P, :],
+                nc.scalar.copy,
+            )
+            if q == HALF_BLOCKS - 1:
+                x_codes[half] = codes.tile([P, PASSES * N_MOVE], U32, align_bytes=64, name="x_codes")
+                x_scales[half] = codes.tile([P, PASSES * N_MOVE], U8, align_bytes=64, name="x_scales")
+                nc.vector.quantize_mx(
+                    out=x_codes[half][:].bitcast(FP8X4), scales=x_scales[half][:], in_=x_grouped[half][:]
+                )
+
+        y_rows = {}
+
+        def product_and_conv(b, e):
+            acc = []
+            for h in range(T_HALVES):
+                bank = accs.tile([P, N_MOVE], F32, name="acc")
+                half = b * T_HALVES + h
+                for g in range(PASSES):
+                    w_cols = slice((e * PASSES + g) * P, (e * PASSES + g + 1) * P)
+                    x_cols = slice(g * N_MOVE, (g + 1) * N_MOVE)
+                    nc.tensor.matmul_mx(
+                        out=bank[:],
+                        lhsT=w_codes[:, w_cols].bitcast(FP8X4),
+                        lhsT_scale=w_scales[:, w_cols],
+                        rhs=x_codes[half][:, x_cols].bitcast(FP8X4),
+                        rhs_scale=x_scales[half][:, x_cols],
+                        start=(g == 0),
+                        stop=(g == PASSES - 1),
+                    )
+                acc.append(bank)
+            y = ys.tile([P, T], F32, name="y")
+            y_rows[(b, e)] = y
+            for h in range(T_HALVES):
+                nc.scalar.activation(
+                    out=y[:, h * N_MOVE : (h + 1) * N_MOVE],
+                    in_=acc[h][:],
+                    func=ACT.Identity,
+                    bias=bias_all[:, e : e + 1],
+                    scale=chan[:, 3, e : e + 1],
+                )
+            for j in (0, KW - 1):
+                shift = j - 1
+                for h in range(T_HALVES):
+                    src_lo = max(h * N_MOVE, shift)
+                    src_hi = min((h + 1) * N_MOVE, T + shift)
+                    nc.vector.scalar_tensor_tensor(
+                        out=y[:, src_lo - shift : src_hi - shift],
+                        in0=acc[h][:, src_lo - h * N_MOVE : src_hi - h * N_MOVE],
+                        scalar=chan[:, 2 + j, e : e + 1],
+                        in1=y[:, src_lo - shift : src_hi - shift],
+                        op0=ALU.mult,
+                        op1=ALU.add,
+                    )
+            nc.gpsimd.tensor_tensor(
+                out=y[:, 0 : T : T - 1], in0=y[:, 0 : T : T - 1], in1=edge_fix[:, e, :], op=ALU.add
+            )
+
+        def store_block(m, vector_helps):
+            b, k = divmod(m, T_BLOCKS)
+            out_rows = outs.tile([P, D], F32)
+            for bank_no in range(D_TILES // BANK_TILES):
+                back = backs.tile([P, N_MOVE], F32)
+                for i in range(BANK_TILES):
+                    nc.tensor.transpose(
+                        back[:, i * P : (i + 1) * P],
+                        y_rows[(b, bank_no * BANK_TILES + i)][:, k * P : (k + 1) * P],
+                        ident[:],
+                    )
+                copy = nc.vector.tensor_copy if (vector_helps and bank_no == 1) else nc.scalar.copy
+                copy(out=out_rows[:, bank_no * N_MOVE : (bank_no + 1) * N_MOVE], in_=back[:])
+            nc.sync.dma_start(out=out[b, k * P : (k + 1) * P, :], in_=out_rows[:])
+
+        for e in range(W_AHEAD):
+            prepare_w(e)
+        for n in range(X_AHEAD):
+            prepare_x(n)
+        for s in range(CONV_STEPS + Y_LAG):
+            if s < CONV_STEPS:
+                product_and_conv(s // D_TILES, s % D_TILES)
+            if s >= Y_LAG:
+                store_block(s - Y_LAG, s >= CONV_STEPS)
+            if s + X_AHEAD < B * T_BLOCKS:
+                prepare_x(s + X_AHEAD)
+            if s + W_AHEAD < D_TILES:
+                prepare_w(s + W_AHEAD)

@@ -17,24 +17,27 @@ PACK = 4
 K_PASS = P * PACK
 PASSES = C // K_PASS
 PAIRS = PACK // 2
-N_MOVE = 512
-T_HALVES = T // N_MOVE
+BANK = 512
+T_HALVES = T // BANK
 T_BLOCKS = T // P
-HALF_BLOCKS = N_MOVE // P
+X_BLOCKS = B * T_BLOCKS
+BANK_BLOCKS = BANK // P
 D_TILES = D // P
-BANK_TILES = N_MOVE // P
 LOAD_BLOCKS = 2
+STORE_BLOCKS = 2
+GROUP_STORES = T_BLOCKS // STORE_BLOCKS
 
-X_AHEAD = T_BLOCKS + 2
+STEPS = B * D_TILES
+X_AHEAD = T_BLOCKS + 1
 W_AHEAD = 2
-Y_LAG = T_BLOCKS + 1
-CONV_STEPS = B * D_TILES
+STORE_LAG = BANK_BLOCKS + 1
+VECTOR_EVERY = 3
 
 FLOPS = 2 * B * T * C * D + 2 * KW * B * T * D
 
 
-def flip_block(nc, flips, ident, words, grouped_words, copy):
-    flipped = flips.tile([P, PASSES, PAIRS, P], F32, tag="flip")
+def flip_block(nc, turns, ident, words, grouped_words, copy):
+    flipped = turns.tile([P, PASSES, PAIRS, P], F32, tag="turn")
     for g in range(PASSES):
         for u in range(PAIRS):
             first = (g * PAIRS + u) * P
@@ -45,20 +48,21 @@ def flip_block(nc, flips, ident, words, grouped_words, copy):
 def tile_cvim_pa_t_kernel(tc, x, w1, b1, w2, b2, out):
     nc = tc.nc
     with ExitStack() as pools:
+        pools.enter_context(tc.manual_schedule())
         consts = pools.enter_context(tc.tile_pool(name="consts", bufs=1))
         raws = pools.enter_context(tc.tile_pool(name="raws", bufs=1))
         groups = pools.enter_context(tc.tile_pool(name="groups", bufs=2))
         codes = pools.enter_context(tc.tile_pool(name="codes", bufs=2 * T_HALVES))
-        ys = pools.enter_context(tc.tile_pool(name="ys", bufs=D_TILES + Y_LAG))
+        ys = pools.enter_context(tc.tile_pool(name="ys", bufs=BANK_BLOCKS + STORE_LAG))
         outs = pools.enter_context(tc.tile_pool(name="outs", bufs=4))
-        accs = pools.enter_context(tc.psum_pool(name="accs", bufs=4))
-        flips = pools.enter_context(tc.psum_pool(name="flips", bufs=2))
-        backs = pools.enter_context(tc.psum_pool(name="backs", bufs=2))
+        accs = pools.enter_context(tc.psum_pool(name="accs", bufs=5))
+        turns = pools.enter_context(tc.psum_pool(name="turns", bufs=3))
 
         ident = consts.tile([P, P], F32)
         make_identity(nc, ident[:])
 
-        x_raw = [raws.tile([P, T_BLOCKS * C], BF16, name="x_raw%d" % b) for b in range(B)]
+        x_rows = x.flatten_outer_dims()
+        x_raw = raws.tile([P, X_BLOCKS * C], BF16)
         w_raw = raws.tile([P, D_TILES * C], BF16)
 
         def load_rows(raw, rows, first):
@@ -75,19 +79,13 @@ def tile_cvim_pa_t_kernel(tc, x, w1, b1, w2, b2, out):
             out=rows_bf16[0:D_TILES, 2 * P : (2 + KW) * P], in_=w2.rearrange("(e p) j -> e (p j)", p=P)
         )
 
-        load_rows(x_raw[0], x[0], 0)
-        load_rows(x_raw[0], x[0], 2)
-        load_rows(w_raw, w1, 0)
-        load_rows(x_raw[0], x[0], 4)
-        load_rows(x_raw[0], x[0], 6)
-        load_rows(x_raw[1], x[1], 0)
-        for first in range(LOAD_BLOCKS, D_TILES, LOAD_BLOCKS):
+        for first in range(0, T_BLOCKS, LOAD_BLOCKS):
+            load_rows(x_raw, x_rows, first)
+        for first in range(0, D_TILES, LOAD_BLOCKS):
             load_rows(w_raw, w1, first)
-        for first in range(LOAD_BLOCKS, T_BLOCKS, LOAD_BLOCKS):
-            load_rows(x_raw[1], x[1], first)
-        for b in range(2, B):
-            for first in range(0, T_BLOCKS, LOAD_BLOCKS):
-                load_rows(x_raw[b], x[b], first)
+            load_rows(x_raw, x_rows, T_BLOCKS + first)
+        for first in range(2 * T_BLOCKS, X_BLOCKS, LOAD_BLOCKS):
+            load_rows(x_raw, x_rows, first)
 
         rows_f32 = consts.tile([P, 2 + KW, P], F32)
         nc.vector.tensor_copy(
@@ -99,7 +97,7 @@ def tile_cvim_pa_t_kernel(tc, x, w1, b1, w2, b2, out):
         )
         chan = consts.tile([P, 2 + KW, D_TILES], F32)
         for v in range(2 + KW):
-            column = flips.tile([P, P], F32, tag="flip")
+            column = turns.tile([P, P], F32, tag="turn")
             nc.tensor.transpose(column[:], rows_f32[:, v, :], ident[:])
             nc.vector.tensor_copy(out=chan[:, v, :], in_=column[:, 0:D_TILES])
         bias1 = chan[:, 0, :]
@@ -123,60 +121,63 @@ def tile_cvim_pa_t_kernel(tc, x, w1, b1, w2, b2, out):
 
         w_codes = consts.tile([P, D_TILES * PASSES * P], U32, align_bytes=64)
         w_scales = consts.tile([P, D_TILES * PASSES * P], U8, align_bytes=64)
+        w_grouped = {}
 
-        def prepare_w(e):
-            w_grouped = groups.tile([P, PASSES * P * PACK], BF16, align_bytes=64)
+        def flip_w(e):
+            w_grouped[e] = groups.tile([P, PASSES * P * PACK], BF16, align_bytes=64, name="w_grouped")
             flip_block(
                 nc,
-                flips,
+                turns,
                 ident,
                 w_raw[:].bitcast(F32)[:, e * (C // 2) : (e + 1) * (C // 2)],
-                w_grouped[:].bitcast(F32).rearrange("p (g r u) -> p g r u", g=PASSES, u=PAIRS),
+                w_grouped[e][:].bitcast(F32).rearrange("p (g r u) -> p g r u", g=PASSES, u=PAIRS),
                 nc.scalar.copy,
             )
+
+        def quantise_w(e):
             cols = slice(e * PASSES * P, (e + 1) * PASSES * P)
             nc.vector.quantize_mx(
-                out=w_codes[:, cols].bitcast(FP8X4), scales=w_scales[:, cols], in_=w_grouped[:]
+                out=w_codes[:, cols].bitcast(FP8X4), scales=w_scales[:, cols], in_=w_grouped[e][:]
             )
 
         x_grouped = {}
         x_codes = {}
         x_scales = {}
 
-        def prepare_x(n):
-            half, q = divmod(n, HALF_BLOCKS)
-            b, k = divmod(n, T_BLOCKS)
+        def flip_x(n):
+            half, q = divmod(n, BANK_BLOCKS)
             if q == 0:
                 x_grouped[half] = groups.tile(
-                    [P, PASSES * N_MOVE * PACK], BF16, align_bytes=64, name="x_grouped"
+                    [P, PASSES * BANK * PACK], BF16, align_bytes=64, name="x_grouped"
                 )
             flip_block(
                 nc,
-                flips,
+                turns,
                 ident,
-                x_raw[b][:].bitcast(F32)[:, k * (C // 2) : (k + 1) * (C // 2)],
+                x_raw[:].bitcast(F32)[:, n * (C // 2) : (n + 1) * (C // 2)],
                 x_grouped[half][:]
                 .bitcast(F32)
                 .rearrange("p (g t u) -> p g t u", g=PASSES, u=PAIRS)[:, :, q * P : (q + 1) * P, :],
-                nc.scalar.copy,
+                nc.vector.tensor_copy if n % VECTOR_EVERY == VECTOR_EVERY - 1 else nc.scalar.copy,
             )
-            if q == HALF_BLOCKS - 1:
-                x_codes[half] = codes.tile([P, PASSES * N_MOVE], U32, align_bytes=64, name="x_codes")
-                x_scales[half] = codes.tile([P, PASSES * N_MOVE], U8, align_bytes=64, name="x_scales")
-                nc.vector.quantize_mx(
-                    out=x_codes[half][:].bitcast(FP8X4), scales=x_scales[half][:], in_=x_grouped[half][:]
-                )
+
+        def quantise_x(half):
+            x_codes[half] = codes.tile([P, PASSES * BANK], U32, align_bytes=64, name="x_codes")
+            x_scales[half] = codes.tile([P, PASSES * BANK], U8, align_bytes=64, name="x_scales")
+            nc.vector.quantize_mx(
+                out=x_codes[half][:].bitcast(FP8X4), scales=x_scales[half][:], in_=x_grouped[half][:]
+            )
 
         y_rows = {}
 
         def product_and_conv(b, e):
             acc = []
             for h in range(T_HALVES):
-                bank = accs.tile([P, N_MOVE], F32, name="acc")
+                bank = accs.tile([P, BANK], F32, name="acc")
                 half = b * T_HALVES + h
                 for g in range(PASSES):
                     w_cols = slice((e * PASSES + g) * P, (e * PASSES + g + 1) * P)
-                    x_cols = slice(g * N_MOVE, (g + 1) * N_MOVE)
+                    x_cols = slice(g * BANK, (g + 1) * BANK)
                     nc.tensor.matmul_mx(
                         out=bank[:],
                         lhsT=w_codes[:, w_cols].bitcast(FP8X4),
@@ -191,7 +192,7 @@ def tile_cvim_pa_t_kernel(tc, x, w1, b1, w2, b2, out):
             y_rows[(b, e)] = y
             for h in range(T_HALVES):
                 nc.scalar.activation(
-                    out=y[:, h * N_MOVE : (h + 1) * N_MOVE],
+                    out=y[:, h * BANK : (h + 1) * BANK],
                     in_=acc[h][:],
                     func=ACT.Identity,
                     bias=bias_all[:, e : e + 1],
@@ -200,11 +201,11 @@ def tile_cvim_pa_t_kernel(tc, x, w1, b1, w2, b2, out):
             for j in (0, KW - 1):
                 shift = j - 1
                 for h in range(T_HALVES):
-                    src_lo = max(h * N_MOVE, shift)
-                    src_hi = min((h + 1) * N_MOVE, T + shift)
+                    src_lo = max(h * BANK, shift)
+                    src_hi = min((h + 1) * BANK, T + shift)
                     nc.vector.scalar_tensor_tensor(
                         out=y[:, src_lo - shift : src_hi - shift],
-                        in0=acc[h][:, src_lo - h * N_MOVE : src_hi - h * N_MOVE],
+                        in0=acc[h][:, src_lo - h * BANK : src_hi - h * BANK],
                         scalar=chan[:, 2 + j, e : e + 1],
                         in1=y[:, src_lo - shift : src_hi - shift],
                         op0=ALU.mult,
@@ -214,31 +215,41 @@ def tile_cvim_pa_t_kernel(tc, x, w1, b1, w2, b2, out):
                 out=y[:, 0 : T : T - 1], in0=y[:, 0 : T : T - 1], in1=edge_fix[:, e, :], op=ALU.add
             )
 
-        def store_block(m, vector_helps):
-            b, k = divmod(m, T_BLOCKS)
-            out_rows = outs.tile([P, D], F32)
-            for bank_no in range(D_TILES // BANK_TILES):
-                back = backs.tile([P, N_MOVE], F32)
-                for i in range(BANK_TILES):
+        def store(r, vector_helps):
+            group, pair = divmod(r, GROUP_STORES)
+            b, d_half = divmod(group, D_TILES // BANK_BLOCKS)
+            out_rows = outs.tile([P, STORE_BLOCKS, BANK], F32)
+            for i in range(STORE_BLOCKS):
+                k = pair * STORE_BLOCKS + i
+                back = turns.tile([P, BANK], F32, tag="turn")
+                for m in range(BANK_BLOCKS):
                     nc.tensor.transpose(
-                        back[:, i * P : (i + 1) * P],
-                        y_rows[(b, bank_no * BANK_TILES + i)][:, k * P : (k + 1) * P],
+                        back[:, m * P : (m + 1) * P],
+                        y_rows[(b, d_half * BANK_BLOCKS + m)][:, k * P : (k + 1) * P],
                         ident[:],
                     )
-                copy = nc.vector.tensor_copy if (vector_helps and bank_no == 1) else nc.scalar.copy
-                copy(out=out_rows[:, bank_no * N_MOVE : (bank_no + 1) * N_MOVE], in_=back[:])
-            nc.sync.dma_start(out=out[b, k * P : (k + 1) * P, :], in_=out_rows[:])
+                copy = nc.vector.tensor_copy if (vector_helps and i == 1) else nc.scalar.copy
+                copy(out=out_rows[:, i, :], in_=back[:])
+            t_lo = pair * STORE_BLOCKS * P
+            nc.sync.dma_start(
+                out=out[b, t_lo : t_lo + STORE_BLOCKS * P, d_half * BANK : (d_half + 1) * BANK].rearrange(
+                    "(k p) d -> p k d", p=P
+                ),
+                in_=out_rows[:],
+            )
 
-        for e in range(W_AHEAD):
-            prepare_w(e)
-        for n in range(X_AHEAD):
-            prepare_x(n)
-        for s in range(CONV_STEPS + Y_LAG):
-            if s < CONV_STEPS:
+        for s in range(-X_AHEAD, STEPS + STORE_LAG):
+            n = s + X_AHEAD
+            if n % BANK_BLOCKS == 0 and 0 < n <= X_BLOCKS:
+                quantise_x(n // BANK_BLOCKS - 1)
+            e = s + W_AHEAD
+            if 0 < e <= D_TILES:
+                quantise_w(e - 1)
+            if 0 <= s < STEPS:
                 product_and_conv(s // D_TILES, s % D_TILES)
-            if s >= Y_LAG:
-                store_block(s - Y_LAG, s >= CONV_STEPS)
-            if s + X_AHEAD < B * T_BLOCKS:
-                prepare_x(s + X_AHEAD)
-            if s + W_AHEAD < D_TILES:
-                prepare_w(s + W_AHEAD)
+            if s >= STORE_LAG:
+                store(s - STORE_LAG, s >= STEPS)
+            if n < X_BLOCKS:
+                flip_x(n)
+            if 0 <= e < D_TILES:
+                flip_w(e)

@@ -18,31 +18,21 @@ K_PASS = P * PACK
 PASSES = C // K_PASS
 PAIRS = PACK // 2
 BANK = 512
-T_HALVES = T // BANK
+T_BANKS = T // BANK
 T_BLOCKS = T // P
 X_BLOCKS = B * T_BLOCKS
 BANK_BLOCKS = BANK // P
 D_TILES = D // P
 LOAD_BLOCKS = 2
-STORE_BLOCKS = 2
-GROUP_STORES = T_BLOCKS // STORE_BLOCKS
+STORE_TILES = 2
 
 STEPS = B * D_TILES
 X_AHEAD = T_BLOCKS + 1
 W_AHEAD = 2
-STORE_LAG = BANK_BLOCKS + 1
+BACK_LAG = 3
 VECTOR_EVERY = 3
 
 FLOPS = 2 * B * T * C * D + 2 * KW * B * T * D
-
-
-def flip_block(nc, turns, ident, words, grouped_words, copy):
-    flipped = turns.tile([P, PASSES, PAIRS, P], F32, tag="turn")
-    for g in range(PASSES):
-        for u in range(PAIRS):
-            first = (g * PAIRS + u) * P
-            nc.tensor.transpose(flipped[:, g, u, :], words[:, first : first + P], ident[:])
-    copy(out=grouped_words, in_=flipped[:].rearrange("p g u r -> p g r u"))
 
 
 def tile_cvim_pa_t_kernel(tc, x, w1, b1, w2, b2, out):
@@ -52,14 +42,19 @@ def tile_cvim_pa_t_kernel(tc, x, w1, b1, w2, b2, out):
         consts = pools.enter_context(tc.tile_pool(name="consts", bufs=1))
         raws = pools.enter_context(tc.tile_pool(name="raws", bufs=1))
         groups = pools.enter_context(tc.tile_pool(name="groups", bufs=2))
-        codes = pools.enter_context(tc.tile_pool(name="codes", bufs=2 * T_HALVES))
-        ys = pools.enter_context(tc.tile_pool(name="ys", bufs=BANK_BLOCKS + STORE_LAG))
-        outs = pools.enter_context(tc.tile_pool(name="outs", bufs=4))
+        codes = pools.enter_context(tc.tile_pool(name="codes", bufs=2 * T_BANKS))
+        ys = pools.enter_context(tc.tile_pool(name="ys", bufs=BACK_LAG + 2))
+        outs = pools.enter_context(tc.tile_pool(name="outs", bufs=3))
         accs = pools.enter_context(tc.psum_pool(name="accs", bufs=5))
         turns = pools.enter_context(tc.psum_pool(name="turns", bufs=3))
 
-        ident = consts.tile([P, P], F32)
-        make_identity(nc, ident[:])
+        rows_bf16 = consts.tile([P, (2 + KW) * P], BF16)
+        nc.gpsimd.memset(rows_bf16[:], 0.0)
+        nc.sync.dma_start(out=rows_bf16[0:D_TILES, 0:P], in_=b1.rearrange("(e p) -> e p", p=P))
+        nc.sync.dma_start(out=rows_bf16[0:D_TILES, P : 2 * P], in_=b2.rearrange("(e p) -> e p", p=P))
+        nc.sync.dma_start(
+            out=rows_bf16[0:D_TILES, 2 * P : (2 + KW) * P], in_=w2.rearrange("(e p) j -> e (p j)", p=P)
+        )
 
         x_rows = x.flatten_outer_dims()
         x_raw = raws.tile([P, X_BLOCKS * C], BF16)
@@ -71,14 +66,6 @@ def tile_cvim_pa_t_kernel(tc, x, w1, b1, w2, b2, out):
                 in_=rows[first * P : (first + LOAD_BLOCKS) * P, :].rearrange("(k p) c -> p k c", p=P),
             )
 
-        rows_bf16 = consts.tile([P, (2 + KW) * P], BF16)
-        nc.vector.memset(rows_bf16[:], 0.0)
-        nc.scalar.dma_start(out=rows_bf16[0:D_TILES, 0:P], in_=b1.rearrange("(e p) -> e p", p=P))
-        nc.scalar.dma_start(out=rows_bf16[0:D_TILES, P : 2 * P], in_=b2.rearrange("(e p) -> e p", p=P))
-        nc.scalar.dma_start(
-            out=rows_bf16[0:D_TILES, 2 * P : (2 + KW) * P], in_=w2.rearrange("(e p) j -> e (p j)", p=P)
-        )
-
         for first in range(0, T_BLOCKS, LOAD_BLOCKS):
             load_rows(x_raw, x_rows, first)
         for first in range(0, D_TILES, LOAD_BLOCKS):
@@ -86,6 +73,9 @@ def tile_cvim_pa_t_kernel(tc, x, w1, b1, w2, b2, out):
             load_rows(x_raw, x_rows, T_BLOCKS + first)
         for first in range(2 * T_BLOCKS, X_BLOCKS, LOAD_BLOCKS):
             load_rows(x_raw, x_rows, first)
+
+        ident = consts.tile([P, P], F32)
+        make_identity(nc, ident[:])
 
         rows_f32 = consts.tile([P, 2 + KW, P], F32)
         nc.vector.tensor_copy(
@@ -119,20 +109,22 @@ def tile_cvim_pa_t_kernel(tc, x, w1, b1, w2, b2, out):
                 op1=ALU.mult,
             )
 
+        def flip(raw, block):
+            words = raw[:].bitcast(F32)[:, block * (C // 2) : (block + 1) * (C // 2)]
+            flipped = turns.tile([P, PASSES, PAIRS, P], F32, tag="turn")
+            for g in range(PASSES):
+                for u in range(PAIRS):
+                    first = (g * PAIRS + u) * P
+                    nc.tensor.transpose(flipped[:, g, u, :], words[:, first : first + P], ident[:])
+            return flipped
+
+        def regroup(copy, flipped, grouped, rows, first_row):
+            words = grouped[:].bitcast(F32).rearrange("p (g r u) -> p g r u", g=PASSES, r=rows)
+            copy(out=words[:, :, first_row : first_row + P, :], in_=flipped[:].rearrange("p g u r -> p g r u"))
+
         w_codes = consts.tile([P, D_TILES * PASSES * P], U32, align_bytes=64)
         w_scales = consts.tile([P, D_TILES * PASSES * P], U8, align_bytes=64)
         w_grouped = {}
-
-        def flip_w(e):
-            w_grouped[e] = groups.tile([P, PASSES * P * PACK], BF16, align_bytes=64, name="w_grouped")
-            flip_block(
-                nc,
-                turns,
-                ident,
-                w_raw[:].bitcast(F32)[:, e * (C // 2) : (e + 1) * (C // 2)],
-                w_grouped[e][:].bitcast(F32).rearrange("p (g r u) -> p g r u", g=PASSES, u=PAIRS),
-                nc.scalar.copy,
-            )
 
         def quantise_w(e):
             cols = slice(e * PASSES * P, (e + 1) * PASSES * P)
@@ -144,53 +136,33 @@ def tile_cvim_pa_t_kernel(tc, x, w1, b1, w2, b2, out):
         x_codes = {}
         x_scales = {}
 
-        def flip_x(n):
-            half, q = divmod(n, BANK_BLOCKS)
-            if q == 0:
-                x_grouped[half] = groups.tile(
-                    [P, PASSES * BANK * PACK], BF16, align_bytes=64, name="x_grouped"
-                )
-            flip_block(
-                nc,
-                turns,
-                ident,
-                x_raw[:].bitcast(F32)[:, n * (C // 2) : (n + 1) * (C // 2)],
-                x_grouped[half][:]
-                .bitcast(F32)
-                .rearrange("p (g t u) -> p g t u", g=PASSES, u=PAIRS)[:, :, q * P : (q + 1) * P, :],
-                nc.vector.tensor_copy if n % VECTOR_EVERY == VECTOR_EVERY - 1 else nc.scalar.copy,
-            )
-
-        def quantise_x(half):
-            x_codes[half] = codes.tile([P, PASSES * BANK], U32, align_bytes=64, name="x_codes")
-            x_scales[half] = codes.tile([P, PASSES * BANK], U8, align_bytes=64, name="x_scales")
+        def quantise_x(bank_no):
+            x_codes[bank_no] = codes.tile([P, PASSES * BANK], U32, align_bytes=64, name="x_codes")
+            x_scales[bank_no] = codes.tile([P, PASSES * BANK], U8, align_bytes=64, name="x_scales")
             nc.vector.quantize_mx(
-                out=x_codes[half][:].bitcast(FP8X4), scales=x_scales[half][:], in_=x_grouped[half][:]
+                out=x_codes[bank_no][:].bitcast(FP8X4), scales=x_scales[bank_no][:], in_=x_grouped[bank_no][:]
             )
 
-        y_rows = {}
+        def multiply(b, e, h):
+            acc = accs.tile([P, BANK], F32)
+            bank_no = b * T_BANKS + h
+            for g in range(PASSES):
+                w_cols = slice((e * PASSES + g) * P, (e * PASSES + g + 1) * P)
+                x_cols = slice(g * BANK, (g + 1) * BANK)
+                nc.tensor.matmul_mx(
+                    out=acc[:],
+                    lhsT=w_codes[:, w_cols].bitcast(FP8X4),
+                    lhsT_scale=w_scales[:, w_cols],
+                    rhs=x_codes[bank_no][:, x_cols].bitcast(FP8X4),
+                    rhs_scale=x_scales[bank_no][:, x_cols],
+                    start=(g == 0),
+                    stop=(g == PASSES - 1),
+                )
+            return acc
 
-        def product_and_conv(b, e):
-            acc = []
-            for h in range(T_HALVES):
-                bank = accs.tile([P, BANK], F32, name="acc")
-                half = b * T_HALVES + h
-                for g in range(PASSES):
-                    w_cols = slice((e * PASSES + g) * P, (e * PASSES + g + 1) * P)
-                    x_cols = slice(g * BANK, (g + 1) * BANK)
-                    nc.tensor.matmul_mx(
-                        out=bank[:],
-                        lhsT=w_codes[:, w_cols].bitcast(FP8X4),
-                        lhsT_scale=w_scales[:, w_cols],
-                        rhs=x_codes[half][:, x_cols].bitcast(FP8X4),
-                        rhs_scale=x_scales[half][:, x_cols],
-                        start=(g == 0),
-                        stop=(g == PASSES - 1),
-                    )
-                acc.append(bank)
-            y = ys.tile([P, T], F32, name="y")
-            y_rows[(b, e)] = y
-            for h in range(T_HALVES):
+        def convolve(e, acc):
+            y = ys.tile([P, T], F32)
+            for h in range(T_BANKS):
                 nc.scalar.activation(
                     out=y[:, h * BANK : (h + 1) * BANK],
                     in_=acc[h][:],
@@ -200,7 +172,7 @@ def tile_cvim_pa_t_kernel(tc, x, w1, b1, w2, b2, out):
                 )
             for j in (0, KW - 1):
                 shift = j - 1
-                for h in range(T_HALVES):
+                for h in range(T_BANKS):
                     src_lo = max(h * BANK, shift)
                     src_hi = min((h + 1) * BANK, T + shift)
                     nc.vector.scalar_tensor_tensor(
@@ -214,42 +186,70 @@ def tile_cvim_pa_t_kernel(tc, x, w1, b1, w2, b2, out):
             nc.gpsimd.tensor_tensor(
                 out=y[:, 0 : T : T - 1], in0=y[:, 0 : T : T - 1], in1=edge_fix[:, e, :], op=ALU.add
             )
+            return y
 
-        def store(r, vector_helps):
-            group, pair = divmod(r, GROUP_STORES)
-            b, d_half = divmod(group, D_TILES // BANK_BLOCKS)
-            out_rows = outs.tile([P, STORE_BLOCKS, BANK], F32)
-            for i in range(STORE_BLOCKS):
-                k = pair * STORE_BLOCKS + i
-                back = turns.tile([P, BANK], F32, tag="turn")
-                for m in range(BANK_BLOCKS):
-                    nc.tensor.transpose(
-                        back[:, m * P : (m + 1) * P],
-                        y_rows[(b, d_half * BANK_BLOCKS + m)][:, k * P : (k + 1) * P],
-                        ident[:],
-                    )
-                copy = nc.vector.tensor_copy if (vector_helps and i == 1) else nc.scalar.copy
-                copy(out=out_rows[:, i, :], in_=back[:])
-            t_lo = pair * STORE_BLOCKS * P
-            nc.sync.dma_start(
-                out=out[b, t_lo : t_lo + STORE_BLOCKS * P, d_half * BANK : (d_half + 1) * BANK].rearrange(
-                    "(k p) d -> p k d", p=P
-                ),
-                in_=out_rows[:],
-            )
+        def turn_back(y, h):
+            back = turns.tile([P, BANK_BLOCKS, P], F32, tag="turn")
+            for i in range(BANK_BLOCKS):
+                k = h * BANK_BLOCKS + i
+                nc.tensor.transpose(back[:, i, :], y[:, k * P : (k + 1) * P], ident[:])
+            return back
 
-        for s in range(-X_AHEAD, STEPS + STORE_LAG):
+        y_rows = {}
+        out_rows = {}
+        for s in range(-X_AHEAD, STEPS + BACK_LAG):
             n = s + X_AHEAD
+            e_next = s + W_AHEAD
+            done = s - BACK_LAG
+            multiplies = 0 <= s < STEPS
+            b, e = divmod(s, D_TILES)
+
             if n % BANK_BLOCKS == 0 and 0 < n <= X_BLOCKS:
                 quantise_x(n // BANK_BLOCKS - 1)
-            e = s + W_AHEAD
-            if 0 < e <= D_TILES:
-                quantise_w(e - 1)
-            if 0 <= s < STEPS:
-                product_and_conv(s // D_TILES, s % D_TILES)
-            if s >= STORE_LAG:
-                store(s - STORE_LAG, s >= STEPS)
+            if 0 < e_next <= D_TILES:
+                quantise_w(e_next - 1)
+
+            acc = []
+            back = []
+            if multiplies:
+                for h in range(T_BANKS):
+                    acc.append(multiply(b, e, h))
+            if done >= 0:
+                for h in range(T_BANKS):
+                    back.append(turn_back(y_rows[done], h))
             if n < X_BLOCKS:
-                flip_x(n)
-            if 0 <= e < D_TILES:
-                flip_w(e)
+                x_flipped = flip(x_raw, n)
+            if 0 <= e_next < D_TILES:
+                w_flipped = flip(w_raw, e_next)
+
+            if multiplies:
+                y_rows[s] = convolve(e, acc)
+            if done >= 0:
+                pair, j = divmod(done, STORE_TILES)
+                if j == 0:
+                    out_rows[pair] = outs.tile([P, T_BLOCKS, STORE_TILES * P], F32, name="out_rows")
+                for h in range(T_BANKS):
+                    copy = nc.vector.tensor_copy if (h == 1 and not multiplies) else nc.scalar.copy
+                    copy(
+                        out=out_rows[pair][:, h * BANK_BLOCKS : (h + 1) * BANK_BLOCKS, j * P : (j + 1) * P],
+                        in_=back[h][:],
+                    )
+                if j == STORE_TILES - 1:
+                    d_lo = (done % D_TILES - j) * P
+                    nc.sync.dma_start(
+                        out=out[done // D_TILES, :, d_lo : d_lo + STORE_TILES * P].rearrange(
+                            "(k p) d -> p k d", p=P
+                        ),
+                        in_=out_rows[pair][:],
+                    )
+            if n < X_BLOCKS:
+                bank_no, q = divmod(n, BANK_BLOCKS)
+                if q == 0:
+                    x_grouped[bank_no] = groups.tile(
+                        [P, PASSES * BANK * PACK], BF16, align_bytes=64, name="x_grouped"
+                    )
+                copy = nc.vector.tensor_copy if n % VECTOR_EVERY == VECTOR_EVERY - 1 else nc.scalar.copy
+                regroup(copy, x_flipped, x_grouped[bank_no], BANK, q * P)
+            if 0 <= e_next < D_TILES:
+                w_grouped[e_next] = groups.tile([P, PASSES * P * PACK], BF16, align_bytes=64, name="w_grouped")
+                regroup(nc.scalar.copy, w_flipped, w_grouped[e_next], P, 0)

@@ -211,11 +211,10 @@ def tile_cvim_pa_t_kernel(tc, x, w1, b1, w2, b2, out):
 
             acc = []
             back = []
-            if multiplies:
-                for h in range(T_BANKS):
+            for h in range(T_BANKS):
+                if multiplies:
                     acc.append(multiply(b, e, h))
-            if done >= 0:
-                for h in range(T_BANKS):
+                if done >= 0:
                     back.append(turn_back(y_rows[done], h))
             if n < X_BLOCKS:
                 x_flipped = flip(x_raw, n)

from contextlib import ExitStack

import concourse.mybir as mybir
from concourse.masks import make_identity

F32 = mybir.dt.float32
BF16 = mybir.dt.bfloat16
U32 = mybir.dt.uint32
U8 = mybir.dt.uint8
FP8X4 = mybir.dt.float8_e4m3fn_x4
ALU = mybir.AluOpType
ACT = mybir.ActivationFunctionType

B, T, C, D, KW = 4, 1024, 1024, 1024, 3
P = 128
PACK = 4
K_PASS = P * PACK
PASSES = C // K_PASS
PAIRS = PACK // 2
BANK = 512
T_BANKS = T // BANK
T_BLOCKS = T // P
X_BLOCKS = B * T_BLOCKS
BANK_BLOCKS = BANK // P
D_TILES = D // P
LOAD_BLOCKS = 2
STORE_TILES = 2

STEPS = B * D_TILES
X_AHEAD = T_BLOCKS + 1
W_AHEAD = 2
BACK_LAG = 3
VECTOR_EVERY = 3

FLOPS = 2 * B * T * C * D + 2 * KW * B * T * D


def tile_cvim_pa_t_kernel(tc, x, w1, b1, w2, b2, out):
    nc = tc.nc
    with ExitStack() as pools:
        pools.enter_context(tc.manual_schedule())
        consts = pools.enter_context(tc.tile_pool(name="consts", bufs=1))
        raws = pools.enter_context(tc.tile_pool(name="raws", bufs=1))
        groups = pools.enter_context(tc.tile_pool(name="groups", bufs=2))
        codes = pools.enter_context(tc.tile_pool(name="codes", bufs=2 * T_BANKS))
        ys = pools.enter_context(tc.tile_pool(name="ys", bufs=BACK_LAG + 2))
        outs = pools.enter_context(tc.tile_pool(name="outs", bufs=3))
        accs = pools.enter_context(tc.psum_pool(name="accs", bufs=5))
        turns = pools.enter_context(tc.psum_pool(name="turns", bufs=3))

        rows_bf16 = consts.tile([P, (2 + KW) * P], BF16)
        nc.gpsimd.memset(rows_bf16[:], 0.0)
        nc.sync.dma_start(out=rows_bf16[0:D_TILES, 0:P], in_=b1.rearrange("(e p) -> e p", p=P))
        nc.sync.dma_start(out=rows_bf16[0:D_TILES, P : 2 * P], in_=b2.rearrange("(e p) -> e p", p=P))
        nc.sync.dma_start(
            out=rows_bf16[0:D_TILES, 2 * P : (2 + KW) * P], in_=w2.rearrange("(e p) j -> e (p j)", p=P)
        )

        x_rows = x.flatten_outer_dims()
        x_raw = raws.tile([P, X_BLOCKS * C], BF16)
        w_raw = raws.tile([P, D_TILES * C], BF16)

        def load_rows(raw, rows, first):
            nc.sync.dma_start(
                out=raw[:].rearrange("p (k c) -> p k c", c=C)[:, first : first + LOAD_BLOCKS, :],
                in_=rows[first * P : (first + LOAD_BLOCKS) * P, :].rearrange("(k p) c -> p k c", p=P),
            )

        for first in range(0, T_BLOCKS, LOAD_BLOCKS):
            load_rows(x_raw, x_rows, first)
        for first in range(0, D_TILES, LOAD_BLOCKS):
            load_rows(w_raw, w1, first)
            load_rows(x_raw, x_rows, T_BLOCKS + first)
        for first in range(2 * T_BLOCKS, X_BLOCKS, LOAD_BLOCKS):
            load_rows(x_raw, x_rows, first)

        ident = consts.tile([P, P], F32)
        make_identity(nc, ident[:])

        rows_f32 = consts.tile([P, 2 + KW, P], F32)
        nc.vector.tensor_copy(
            out=rows_f32[:, 0:2, :], in_=rows_bf16[:, 0 : 2 * P].rearrange("e (v p) -> e v p", v=2)
        )
        nc.vector.tensor_copy(
            out=rows_f32[:, 2 : 2 + KW, :],
            in_=rows_bf16[:, 2 * P : (2 + KW) * P].rearrange("e (p j) -> e j p", j=KW),
        )
        chan = consts.tile([P, 2 + KW, D_TILES], F32)
        for v in range(2 + KW):
            column = turns.tile([P, P], F32, tag="turn")
            nc.tensor.transpose(column[:], rows_f32[:, v, :], ident[:])
            nc.vector.tensor_copy(out=chan[:, v, :], in_=column[:, 0:D_TILES])
        bias1 = chan[:, 0, :]
        bias2 = chan[:, 1, :]
        tap_sum = consts.tile([P, D_TILES], F32)
        nc.vector.tensor_tensor(out=tap_sum[:], in0=chan[:, 2, :], in1=chan[:, 3, :], op=ALU.add)
        nc.vector.tensor_tensor(out=tap_sum[:], in0=tap_sum[:], in1=chan[:, 4, :], op=ALU.add)
        bias_all = consts.tile([P, D_TILES], F32)
        nc.vector.tensor_tensor(out=bias_all[:], in0=tap_sum[:], in1=bias1, op=ALU.mult)
        nc.vector.tensor_tensor(out=bias_all[:], in0=bias_all[:], in1=bias2, op=ALU.add)
        edge_fix = consts.tile([P, D_TILES, 2], F32)
        for side in range(2):
            nc.vector.scalar_tensor_tensor(
                out=edge_fix[:, :, side],
                in0=bias1,
                scalar=-1.0,
                in1=chan[:, 2 + side * (KW - 1), :],
                op0=ALU.mult,
                op1=ALU.mult,
            )

        def flip(raw, block):
            words = raw[:].bitcast(F32)[:, block * (C // 2) : (block + 1) * (C // 2)]
            flipped = turns.tile([P, PASSES, PAIRS, P], F32, tag="turn")
            for g in range(PASSES):
                for u in range(PAIRS):
                    first = (g * PAIRS + u) * P
                    nc.tensor.transpose(flipped[:, g, u, :], words[:, first : first + P], ident[:])
            return flipped

        def regroup(copy, flipped, grouped, rows, first_row):
            words = grouped[:].bitcast(F32).rearrange("p (g r u) -> p g r u", g=PASSES, r=rows)
            copy(out=words[:, :, first_row : first_row + P, :], in_=flipped[:].rearrange("p g u r -> p g r u"))

        w_codes = consts.tile([P, D_TILES * PASSES * P], U32, align_bytes=64)
        w_scales = consts.tile([P, D_TILES * PASSES * P], U8, align_bytes=64)
        w_grouped = {}

        def quantise_w(e):
            cols = slice(e * PASSES * P, (e + 1) * PASSES * P)
            nc.vector.quantize_mx(
                out=w_codes[:, cols].bitcast(FP8X4), scales=w_scales[:, cols], in_=w_grouped[e][:]
            )

        x_grouped = {}
        x_codes = {}
        x_scales = {}

        def quantise_x(bank_no):
            x_codes[bank_no] = codes.tile([P, PASSES * BANK], U32, align_bytes=64, name="x_codes")
            x_scales[bank_no] = codes.tile([P, PASSES * BANK], U8, align_bytes=64, name="x_scales")
            nc.vector.quantize_mx(
                out=x_codes[bank_no][:].bitcast(FP8X4), scales=x_scales[bank_no][:], in_=x_grouped[bank_no][:]
            )

        def multiply(b, e, h):
            acc = accs.tile([P, BANK], F32)
            bank_no = b * T_BANKS + h
            for g in range(PASSES):
                w_cols = slice((e * PASSES + g) * P, (e * PASSES + g + 1) * P)
                x_cols = slice(g * BANK, (g + 1) * BANK)
                nc.tensor.matmul_mx(
                    out=acc[:],
                    lhsT=w_codes[:, w_cols].bitcast(FP8X4),
                    lhsT_scale=w_scales[:, w_cols],
                    rhs=x_codes[bank_no][:, x_cols].bitcast(FP8X4),
                    rhs_scale=x_scales[bank_no][:, x_cols],
                    start=(g == 0),
                    stop=(g == PASSES - 1),
                )
            return acc

        def convolve(e, acc):
            y = ys.tile([P, T], F32)
            for h in range(T_BANKS):
                nc.scalar.activation(
                    out=y[:, h * BANK : (h + 1) * BANK],
                    in_=acc[h][:],
                    func=ACT.Identity,
                    bias=bias_all[:, e : e + 1],
                    scale=chan[:, 3, e : e + 1],
                )
            for j in (0, KW - 1):
                shift = j - 1
                for h in range(T_BANKS):
                    src_lo = max(h * BANK, shift)
                    src_hi = min((h + 1) * BANK, T + shift)
                    nc.vector.scalar_tensor_tensor(
                        out=y[:, src_lo - shift : src_hi - shift],
                        in0=acc[h][:, src_lo - h * BANK : src_hi - h * BANK],
                        scalar=chan[:, 2 + j, e : e + 1],
                        in1=y[:, src_lo - shift : src_hi - shift],
                        op0=ALU.mult,
                        op1=ALU.add,
                    )
            nc.gpsimd.tensor_tensor(
                out=y[:, 0 : T : T - 1], in0=y[:, 0 : T : T - 1], in1=edge_fix[:, e, :], op=ALU.add
            )
            return y

        def turn_back(y, h):
            back = turns.tile([P, BANK_BLOCKS, P], F32, tag="turn")
            for i in range(BANK_BLOCKS):
                k = h * BANK_BLOCKS + i
                nc.tensor.transpose(back[:, i, :], y[:, k * P : (k + 1) * P], ident[:])
            return back

        y_rows = {}
        out_rows = {}
        for s in range(-X_AHEAD, STEPS + BACK_LAG):
            n = s + X_AHEAD
            e_next = s + W_AHEAD
            done = s - BACK_LAG
            multiplies = 0 <= s < STEPS
            b, e = divmod(s, D_TILES)

            if n % BANK_BLOCKS == 0 and 0 < n <= X_BLOCKS:
                quantise_x(n // BANK_BLOCKS - 1)
            if 0 < e_next <= D_TILES:
                quantise_w(e_next - 1)

            acc = []
            back = []
            for h in range(T_BANKS):
                if multiplies:
                    acc.append(multiply(b, e, h))
                if done >= 0:
                    back.append(turn_back(y_rows[done], h))
            if n < X_BLOCKS:
                x_flipped = flip(x_raw, n)
            if 0 <= e_next < D_TILES:
                w_flipped = flip(w_raw, e_next)

            if multiplies:
                y_rows[s] = convolve(e, acc)
            if done >= 0:
                pair, j = divmod(done, STORE_TILES)
                if j == 0:
                    out_rows[pair] = outs.tile([P, T_BLOCKS, STORE_TILES * P], F32, name="out_rows")
                for h in range(T_BANKS):
                    copy = nc.vector.tensor_copy if (h == 1 and not multiplies) else nc.scalar.copy
                    copy(
                        out=out_rows[pair][:, h * BANK_BLOCKS : (h + 1) * BANK_BLOCKS, j * P : (j + 1) * P],
                        in_=back[h][:],
                    )
                if j == STORE_TILES - 1:
                    d_lo = (done % D_TILES - j) * P
                    nc.sync.dma_start(
                        out=out[done // D_TILES, :, d_lo : d_lo + STORE_TILES * P].rearrange(
                            "(k p) d -> p k d", p=P
                        ),
                        in_=out_rows[pair][:],
                    )
            if n < X_BLOCKS:
                bank_no, q = divmod(n, BANK_BLOCKS)
                if q == 0:
                    x_grouped[bank_no] = groups.tile(
                        [P, PASSES * BANK * PACK], BF16, align_bytes=64, name="x_grouped"
                    )
                copy = nc.vector.tensor_copy if n % VECTOR_EVERY == VECTOR_EVERY - 1 else nc.scalar.copy
                regroup(copy, x_flipped, x_grouped[bank_no], BANK, q * P)
            if 0 <= e_next < D_TILES:
                w_grouped[e_next] = groups.tile([P, PASSES * P * PACK], BF16, align_bytes=64, name="w_grouped")
                regroup(nc.scalar.copy, w_flipped, w_grouped[e_next], P, 0)
